import numpy as np
import ml_dtypes


def mxq(x, axis, fmt="e4m3"):
    dtype, down = {"e4m3": (ml_dtypes.float8_e4m3fn, 7), "e5m2": (ml_dtypes.float8_e5m2, 14)}[fmt]
    v = np.moveaxis(np.asarray(x, np.float32).astype(ml_dtypes.bfloat16).astype(np.float64), axis, -1)
    blocks = v.reshape(v.shape[:-1] + (-1, 32))
    amax = np.abs(blocks).max(-1, keepdims=True)
    byte = np.maximum(np.where(amax > 0, np.frexp(amax)[1] - 1 + 127, 0) - down, 1)
    scale = np.exp2(byte - 127.0)
    codes = (blocks / scale).astype(np.float32).astype(dtype).astype(np.float64)
    return np.moveaxis((codes * scale).reshape(v.shape), -1, axis)


WIDE = False


def mx_kscale(k):
    if not WIDE:
        return np.ones(k)
    levels = np.array([30, -30])
    if k % 512:
        return np.exp2(np.random.permutation(np.resize(levels, k // 32))).repeat(32)
    a = np.empty((k // 512, 16))
    for p in range(k // 512):
        a[p, :8] = np.random.permutation(np.resize(levels, 8))
        for g in range(8):
            far = levels[np.abs(levels - a[p, g]) >= 10]
            a[p, g + 8] = far[np.random.randint(len(far))]
    return np.exp2(a.ravel()).repeat(32)


BF16 = ml_dtypes.bfloat16


def bf(x):
    return np.asarray(x, np.float32).astype(BF16)


def f64(x):
    return np.asarray(x).astype(np.float64)


E2M1 = np.array([0.0, 0.5, 1.0, 1.5, 2.0, 3.0, 4.0, 6.0, -0.0, -0.5, -1.0, -1.5, -2.0, -3.0, -4.0, -6.0])


def pack_weight(w, fmt):
    k, n = w.shape
    w = f64(bf(w)).reshape(k // 32, 32, n)
    amax = np.abs(w).max(1)
    if fmt == "e4m3":
        byte = np.frexp(amax)[1] - 1 + 127 - 7
    else:
        mant, ex = np.frexp(amax / 6.0)
        byte = np.where(mant > 0.5, ex, ex - 1) + 127
    byte = np.clip(np.where(amax > 0, byte, 1), 1, 254)
    scaled = (w * np.exp2(127.0 - byte)[:, None, :]).reshape(k, n).astype(np.float32)
    by_word = np.ascontiguousarray(scaled.reshape(k // 512, 128, 4, n).transpose(0, 1, 3, 2))
    if fmt == "e4m3":
        words = by_word.astype(ml_dtypes.float8_e4m3fn).view(np.uint8)
    else:
        c = by_word.astype(ml_dtypes.float4_e2m1fn).view(np.uint8) & 0xF
        words = c[..., 0::2] | (c[..., 1::2] << 4)
    return np.ascontiguousarray(words), np.ascontiguousarray(byte.astype(np.uint8).reshape(k // 512, 16, n))


def unpack_weight(words, scales, fmt):
    g, p, n, _ = words.shape
    if fmt == "e4m3":
        vals = np.ascontiguousarray(words).view(ml_dtypes.float8_e4m3fn).astype(np.float64)
    else:
        nib = np.empty((g, p, n, 4), np.uint8)
        nib[..., 0::2] = words & 0xF
        nib[..., 1::2] = words >> 4
        vals = E2M1[nib]
    vals = vals * np.repeat(np.exp2(scales.astype(np.float64) - 127.0), 8, axis=1)[..., None]
    return vals.transpose(0, 1, 3, 2).reshape(g * 512, n)

def pack4(w):
    words, scales = pack_weight(w, "e2m1")
    return words.reshape(words.shape[0], 128, -1), scales


def unpack4(words, scales):
    return unpack_weight(words.reshape(words.shape[0], 128, -1, 2), scales, "e2m1")


B, S, H, E, D, TRAIN_LEN = 1, 1024, 1024, 1536, 128, 512


def silu(v):
    return v / (1.0 + np.exp(-v))


def apply_rotary(x, sin, cos):
    x1, x2 = x[..., 0::2], x[..., 1::2]
    return np.concatenate([x1 * cos - x2 * sin, x1 * sin + x2 * cos], axis=-1)


def setup_inputs():
    s = mx_kscale(H)
    pos = np.arange(S)[:, None]
    inv = np.exp(-np.arange(0, D, 2) / D * np.log(10000.0))
    ang = pos * inv[None, :]
    hidden_states = bf(np.random.standard_normal((B, S, H)) * s)
    words, scales = pack4(np.random.standard_normal((H, 2 * E + D)) / np.sqrt(H) / s[:, None])
    return {"hidden_states": hidden_states,
            "sin": bf(np.sin(ang)[None]),
            "cos": bf(np.cos(ang)[None]),
            "W_i_words": words,
            "W_i_scales": scales,
            "q_scale": bf(1.0 + 0.1 * np.random.standard_normal(D)),
            "k_scale": bf(1.0 + 0.1 * np.random.standard_normal(D))}


def reference(hidden_states, sin, cos, W_i_words, W_i_scales, q_scale, k_scale):
    x = silu(mxq(f64(hidden_states), 2, "e5m2") @ unpack4(W_i_words, W_i_scales))
    u, v, qk = np.split(x, [E, 2 * E], axis=-1)
    sn, cs = f64(sin), f64(cos)
    q = apply_rotary(qk * f64(q_scale), sn, cs)
    k = apply_rotary(qk * f64(k_scale), sn, cs)
    return u, v, q, k

@@ -1,0 +1,281 @@
+from contextlib import ExitStack
+
+import concourse.mybir as mybir
+from concourse.masks import make_identity
+
+F32 = mybir.dt.float32
+BF16 = mybir.dt.bfloat16
+U32 = mybir.dt.uint32
+U8 = mybir.dt.uint8
+I32 = mybir.dt.int32
+E5X4 = mybir.dt.float8_e5m2_x4
+E2X4 = mybir.dt.float4_e2m1fn_x4
+ACT = mybir.ActivationFunctionType
+ALU = mybir.AluOpType
+
+S, H, E, D = 1024, 1024, 1536, 128
+P = 128
+MT = S // P
+G = H // 512
+NT = 512
+HALF = D // 2
+
+FLOPS = 2 * S * H * (2 * E + D)
+
+MANUAL = True
+
+CHUNKS = ((0, 512), (512, 1536), (1536, 3200))
+XLOADS = ((0, 1), (1, 1), (2, 2), (4, 2), (6, 2))
+
+
+def chunk_of(col):
+    for c, (c0, c1) in enumerate(CHUNKS):
+        if c0 <= col < c1:
+            return c, col - c0
+    raise ValueError("column outside W_i")
+
+
+def tile_gatedattentionunit_pa_kernel(
+    tc, hidden_states, sin, cos, W_i_words, W_i_scales, q_scale, k_scale, out_0, out_1, out_2, out_3
+):
+    nc = tc.nc
+    x_hbm = hidden_states.flatten_outer_dims().rearrange("(p m) k -> p m k", m=MT)
+    sin_hbm = sin.flatten_outer_dims().rearrange("(p m) i -> p m i", m=MT)
+    cos_hbm = cos.flatten_outer_dims().rearrange("(p m) i -> p m i", m=MT)
+    uv_hbm = [o.flatten_outer_dims().rearrange("(p m) e -> p m e", m=MT) for o in (out_0, out_1)]
+    qk_hbm = [o.flatten_outer_dims().rearrange("(p m) d -> p m d", m=MT) for o in (out_2, out_3)]
+
+    with ExitStack() as ctx:
+        if MANUAL:
+            ctx.enter_context(tc.manual_schedule())
+        const = ctx.enter_context(tc.tile_pool(name="const", bufs=1))
+        stage = ctx.enter_context(tc.tile_pool(name="stage", bufs=4))
+        ep = ctx.enter_context(tc.tile_pool(name="ep", bufs=2))
+        psum = ctx.enter_context(tc.psum_pool(name="psum", bufs=8))
+
+        warm_in = const.tile([P, 1], F32, name="warm_in")
+        warm_out = const.tile([P, 1], F32, name="warm_out")
+        nc.vector.memset(warm_in[:], 0.0)
+        nc.scalar.activation(out=warm_out[:], in_=warm_in[:], func=ACT.Silu)
+
+        planes = []
+        words = []
+        for c, (c0, c1) in enumerate(CHUNKS):
+            plane = const.tile([P, G, c1 - c0], U8, name="plane%d" % c, align_bytes=64)
+            nc.vector.memset(plane[:].bitcast(I32), 0)
+            planes.append(plane)
+            wtile = const.tile([P, G, 2 * (c1 - c0)], U8, name="words%d" % c, align_bytes=64)
+            words.append(wtile)
+
+        ident = const.tile([P, P], F32, name="ident")
+        make_identity(nc, ident[:])
+        ones = const.tile([P, P], BF16, name="ones")
+        nc.vector.memset(ones[:], 1.0)
+        gain_rows = const.tile([P, 2 * D], BF16, name="gain_rows")
+        nc.vector.memset(gain_rows[:], 0.0)
+
+        xc = const.tile([P, G, S], U32, name="xc", align_bytes=64)
+        xs = const.tile([P, G, S], U8, name="xs", align_bytes=64)
+        cos_sb = const.tile([P, MT, HALF], BF16, name="cos_sb")
+        sin_sb = const.tile([P, MT, HALF], BF16, name="sin_sb")
+        gains = const.tile([P, 2, D], F32, name="gains")
+
+        xsrc = {}
+
+        def load_x(i):
+            m0, n = XLOADS[i]
+            xt = const.tile([P, n, H], BF16, name="x%d" % m0)
+            nc.sync.dma_start(out=xt[:], in_=x_hbm[:, m0 : m0 + n, :])
+            for k in range(n):
+                xsrc[m0 + k] = xt[:, k, :]
+
+        def load_w(c):
+            c0, c1 = CHUNKS[c]
+            for q in range(4):
+                nc.sync.dma_start(
+                    out=planes[c][32 * q : 32 * q + 4, :, :].bitcast(I32),
+                    in_=W_i_scales[:, 4 * q : 4 * q + 4, c0:c1].rearrange("g r n -> r g n").bitcast(I32),
+                )
+            nc.sync.dma_start(
+                out=words[c][:].bitcast(I32),
+                in_=W_i_words[:, :, 2 * c0 : 2 * c1].rearrange("g p b -> p g b").bitcast(I32),
+            )
+
+        load_x(0)
+        load_w(0)
+        load_x(1)
+        load_x(2)
+        load_w(1)
+        load_x(3)
+        load_x(4)
+        load_w(2)
+        nc.sync.dma_start(out=gain_rows[0:1, 0:D], in_=q_scale.unsqueeze(0))
+        nc.sync.dma_start(out=gain_rows[0:1, D : 2 * D], in_=k_scale.unsqueeze(0))
+        nc.sync.dma_start(out=cos_sb[:], in_=cos_hbm)
+        nc.sync.dma_start(out=sin_sb[:], in_=sin_hbm)
+
+        xts = {}
+        gxs = {}
+
+        def transpose_x(m):
+            xt = psum.tile([P, 2 * G, P], F32, name="xt%d" % m, tag="bank")
+            w = xsrc[m].bitcast(F32)
+            for g in range(G):
+                for u in range(2):
+                    nc.tensor.transpose(xt[:, 2 * g + u, :], w[:, 256 * g + u : 256 * (g + 1) : 2], ident[:])
+            xts[m] = xt
+
+        def copy_x(m):
+            gx = stage.tile([P, G, P, 2], F32, name="gx%d" % m, tag="gx", align_bytes=64)
+            nc.vector.tensor_copy(out=gx[:], in_=xts[m][:].rearrange("p (g u) r -> p g r u", u=2))
+            gxs[m] = gx
+
+        def quant_x(m):
+            cols = slice(P * m, P * (m + 1))
+            for g in range(G):
+                nc.vector.quantize_mx(
+                    out=xc[:, g, cols].bitcast(E5X4),
+                    scales=xs[:, g, cols],
+                    in_=gxs[m][:, g, :, :].rearrange("p r u -> p (r u)").bitcast(BF16),
+                )
+
+        outs = {}
+
+        def mx(m, j):
+            c, off = chunk_of(NT * j)
+            acc = psum.tile([P, NT], F32, name="acc%d_%d" % (m, j), tag="bank")
+            for g in range(G):
+                nc.tensor.matmul_mx(
+                    out=acc[:],
+                    lhsT=xc[:, g, P * m : P * (m + 1)].bitcast(E5X4),
+                    lhsT_scale=xs[:, g, P * m : P * (m + 1)],
+                    rhs=words[c][:, g, 2 * off : 2 * (off + NT)].bitcast(E2X4),
+                    rhs_scale=planes[c][:, g, off : off + NT],
+                    start=(g == 0),
+                    stop=(g == G - 1),
+                )
+            h, jj = divmod(j, 3)
+            if jj == 0:
+                ot = const.tile([P, E], F32, name="o%d_%d" % (m, h))
+                outs[(m, h)] = ot
+            ot = outs[(m, h)]
+            nc.scalar.activation(out=ot[:, NT * jj : NT * (jj + 1)], in_=acc[:], func=ACT.Silu)
+            if m == MT - 1 and h == 1:
+                if jj >= 1:
+                    lo = 0 if jj == 1 else 2 * NT
+                    nc.sync.dma_start(out=uv_hbm[h][:, m, lo : NT * (jj + 1)], in_=ot[:, lo : NT * (jj + 1)])
+            elif jj == 2:
+                nc.sync.dma_start(out=uv_hbm[h][:, m, :], in_=ot[:])
+
+        qkT = {}
+
+        def mx_qk(mg):
+            c, off = chunk_of(2 * E)
+            acc = psum.tile([P, NT], F32, name="qkacc%d" % mg, tag="bank")
+            for g in range(G):
+                nc.tensor.matmul_mx(
+                    out=acc[:],
+                    lhsT=words[c][:, g, 2 * off : 2 * (off + D)].bitcast(E2X4),
+                    lhsT_scale=planes[c][:, g, off : off + D],
+                    rhs=xc[:, g, NT * mg : NT * (mg + 1)].bitcast(E5X4),
+                    rhs_scale=xs[:, g, NT * mg : NT * (mg + 1)],
+                    start=(g == 0),
+                    stop=(g == G - 1),
+                )
+            st = ep.tile([P, NT], F32, name="qkT%d" % mg, tag="qkT")
+            nc.scalar.activation(out=st[:], in_=acc[:], func=ACT.Silu)
+            qkT[mg] = st
+
+        ys = {}
+
+        def back_transpose(mg):
+            tb = psum.tile([P, 4, D], F32, name="tb%d" % mg, tag="bank")
+            for i in range(4):
+                nc.tensor.transpose(tb[:, i, :], qkT[mg][:, P * i : P * (i + 1)], ident[:])
+            return tb
+
+        def apply_gains(mg, tb):
+            y = ep.tile([P, 2, 4, D], F32, name="y%d" % mg, tag="y")
+            for s in range(2):
+                nc.vector.tensor_tensor(
+                    out=y[:, s, :, :],
+                    in0=tb[:],
+                    in1=gains[:, s, :].unsqueeze(1).to_broadcast([P, 4, D]),
+                    op=ALU.mult,
+                )
+            ys[mg] = y
+
+        def rotate(mg):
+            pairs = ys[mg][:].rearrange("p s m (i e) -> p s m i e", e=2)
+            even = pairs[:, :, :, :, 0]
+            odd = pairs[:, :, :, :, 1]
+            shape = [P, 2, 4, HALF]
+            cb = cos_sb[:, 4 * mg : 4 * mg + 4, :].unsqueeze(1).to_broadcast(shape)
+            sb = sin_sb[:, 4 * mg : 4 * mg + 4, :].unsqueeze(1).to_broadcast(shape)
+            o = ep.tile([P, 2, 4, D], F32, name="rot%d" % mg, tag="rot")
+            t1 = ep.tile(shape, F32, name="t1_%d" % mg, tag="t1")
+            t2 = ep.tile(shape, F32, name="t2_%d" % mg, tag="t2")
+            t3 = ep.tile(shape, F32, name="t3_%d" % mg, tag="t3")
+            t4 = ep.tile(shape, F32, name="t4_%d" % mg, tag="t4")
+            nc.vector.tensor_tensor(out=t1[:], in0=even, in1=cb, op=ALU.mult)
+            nc.vector.tensor_tensor(out=t2[:], in0=odd, in1=sb, op=ALU.mult)
+            nc.vector.tensor_tensor(out=t3[:], in0=even, in1=sb, op=ALU.mult)
+            nc.vector.tensor_tensor(out=t4[:], in0=odd, in1=cb, op=ALU.mult)
+            nc.vector.tensor_tensor(out=o[:, :, :, 0:HALF], in0=t1[:], in1=t2[:], op=ALU.subtract)
+            nc.vector.tensor_tensor(out=o[:, :, :, HALF:D], in0=t3[:], in1=t4[:], op=ALU.add)
+            for s in range(2):
+                nc.gpsimd.dma_start(out=qk_hbm[s][:, 4 * mg : 4 * mg + 4, :], in_=o[:, s, :, :])
+
+        transpose_x(0)
+        copy_x(0)
+        quant_x(0)
+        transpose_x(1)
+        copy_x(1)
+        quant_x(1)
+        mx(0, 0)
+        transpose_x(2)
+        transpose_x(3)
+        copy_x(2)
+        copy_x(3)
+        quant_x(2)
+        quant_x(3)
+        mx(1, 0)
+        mx(2, 0)
+        mx(3, 0)
+        for m in (0, 1):
+            mx(m, 1)
+            mx(m, 2)
+        for m in (4, 5, 6, 7):
+            transpose_x(m)
+        gb = psum.tile([P, NT], F32, name="gb", tag="bank")
+        nc.tensor.matmul(out=gb[:, 0 : 2 * D], lhsT=ones[:], rhs=gain_rows[:], start=True, stop=True)
+        copy_x(4)
+        copy_x(5)
+        quant_x(4)
+        copy_x(6)
+        quant_x(5)
+        copy_x(7)
+        quant_x(6)
+        quant_x(7)
+        nc.vector.tensor_copy(out=gains[:].rearrange("p s d -> p (s d)"), in_=gb[:, 0 : 2 * D])
+        for m in (2, 3):
+            mx(m, 1)
+            mx(m, 2)
+        mx_qk(0)
+        for j in (3, 4, 5):
+            mx(0, j)
+        mx_qk(1)
+        for m in (1, 2):
+            for j in (3, 4, 5):
+                mx(m, j)
+        tb0 = back_transpose(0)
+        tb1 = back_transpose(1)
+        apply_gains(0, tb0)
+        apply_gains(1, tb1)
+        for j in (3, 4, 5):
+            mx(3, j)
+        rotate(0)
+        rotate(1)
+        for m in (4, 5, 6, 7):
+            for j in range(6):
+                mx(m, j)

@@ -23,6 +23,10 @@ HALF = D // 2
 FLOPS = 2 * S * H * (2 * E + D)
 
 MANUAL = True
+BY_R = True
+PRE = (4, 5, 6, 7)
+WARM_HEAD = 0
+WARM_GAP = 0
 
 CHUNKS = ((0, 512), (512, 1536), (1536, 3200))
 XLOADS = ((0, 1), (1, 1), (2, 2), (4, 2), (6, 2))
@@ -57,6 +61,10 @@ def tile_gatedattentionunit_pa_kernel(
         warm_out = const.tile([P, 1], F32, name="warm_out")
         nc.vector.memset(warm_in[:], 0.0)
         nc.scalar.activation(out=warm_out[:], in_=warm_in[:], func=ACT.Silu)
+        ones = const.tile([P, P], BF16, name="ones")
+        nc.vector.memset(ones[:], 1.0)
+        gain_rows = const.tile([P, 2 * D], BF16, name="gain_rows")
+        nc.vector.memset(gain_rows[:], 0.0)
 
         planes = []
         words = []
@@ -69,10 +77,8 @@ def tile_gatedattentionunit_pa_kernel(
 
         ident = const.tile([P, P], F32, name="ident")
         make_identity(nc, ident[:])
-        ones = const.tile([P, P], BF16, name="ones")
-        nc.vector.memset(ones[:], 1.0)
-        gain_rows = const.tile([P, 2 * D], BF16, name="gain_rows")
-        nc.vector.memset(gain_rows[:], 0.0)
+        nc.gpsimd.dma_start(out=gain_rows[0:1, 0:D], in_=q_scale.unsqueeze(0))
+        nc.gpsimd.dma_start(out=gain_rows[0:1, D : 2 * D], in_=k_scale.unsqueeze(0))
 
         xc = const.tile([P, G, S], U32, name="xc", align_bytes=64)
         xs = const.tile([P, G, S], U8, name="xs", align_bytes=64)
@@ -92,37 +98,51 @@ def tile_gatedattentionunit_pa_kernel(
         def load_w(c):
             c0, c1 = CHUNKS[c]
             for q in range(4):
-                nc.sync.dma_start(
-                    out=planes[c][32 * q : 32 * q + 4, :, :].bitcast(I32),
-                    in_=W_i_scales[:, 4 * q : 4 * q + 4, c0:c1].rearrange("g r n -> r g n").bitcast(I32),
-                )
+                if BY_R:
+                    nc.sync.dma_start(
+                        out=planes[c][q : P : 32, :, :].bitcast(I32),
+                        in_=W_i_scales[:, q : 16 : 4, c0:c1].rearrange("g r n -> r g n").bitcast(I32),
+                    )
+                else:
+                    nc.sync.dma_start(
+                        out=planes[c][32 * q : 32 * q + 4, :, :].bitcast(I32),
+                        in_=W_i_scales[:, 4 * q : 4 * q + 4, c0:c1].rearrange("g r n -> r g n").bitcast(I32),
+                    )
             nc.sync.dma_start(
                 out=words[c][:].bitcast(I32),
                 in_=W_i_words[:, :, 2 * c0 : 2 * c1].rearrange("g p b -> p g b").bitcast(I32),
             )
 
         load_x(0)
-        load_w(0)
         load_x(1)
+        load_w(0)
         load_x(2)
         load_w(1)
         load_x(3)
         load_x(4)
         load_w(2)
-        nc.sync.dma_start(out=gain_rows[0:1, 0:D], in_=q_scale.unsqueeze(0))
-        nc.sync.dma_start(out=gain_rows[0:1, D : 2 * D], in_=k_scale.unsqueeze(0))
         nc.sync.dma_start(out=cos_sb[:], in_=cos_hbm)
         nc.sync.dma_start(out=sin_sb[:], in_=sin_hbm)
 
         xts = {}
         gxs = {}
 
+        pres = {}
+
+        def sort_x(m):
+            pre = stage.tile([P, G, 2, P], F32, name="pre%d" % m, tag="pre")
+            nc.vector.tensor_copy(out=pre[:], in_=xsrc[m].bitcast(F32).rearrange("p (g r u) -> p g u r", g=G, u=2))
+            pres[m] = pre
+
         def transpose_x(m):
             xt = psum.tile([P, 2 * G, P], F32, name="xt%d" % m, tag="bank")
             w = xsrc[m].bitcast(F32)
             for g in range(G):
                 for u in range(2):
-                    nc.tensor.transpose(xt[:, 2 * g + u, :], w[:, 256 * g + u : 256 * (g + 1) : 2], ident[:])
+                    if m in PRE:
+                        nc.tensor.transpose(xt[:, 2 * g + u, :], pres[m][:, g, u, :], ident[:])
+                    else:
+                        nc.tensor.transpose(xt[:, 2 * g + u, :], w[:, 256 * g + u : 256 * (g + 1) : 2], ident[:])
             xts[m] = xt
 
         def copy_x(m):
@@ -161,9 +181,8 @@ def tile_gatedattentionunit_pa_kernel(
             ot = outs[(m, h)]
             nc.scalar.activation(out=ot[:, NT * jj : NT * (jj + 1)], in_=acc[:], func=ACT.Silu)
             if m == MT - 1 and h == 1:
-                if jj >= 1:
-                    lo = 0 if jj == 1 else 2 * NT
-                    nc.sync.dma_start(out=uv_hbm[h][:, m, lo : NT * (jj + 1)], in_=ot[:, lo : NT * (jj + 1)])
+                lo = NT * jj
+                nc.sync.dma_start(out=uv_hbm[h][:, m, lo : lo + NT], in_=ot[:, lo : lo + NT])
             elif jj == 2:
                 nc.sync.dma_start(out=uv_hbm[h][:, m, :], in_=ot[:])
 
@@ -205,6 +224,8 @@ def tile_gatedattentionunit_pa_kernel(
                 )
             ys[mg] = y
 
+        rots = {}
+
         def rotate(mg):
             pairs = ys[mg][:].rearrange("p s m (i e) -> p s m i e", e=2)
             even = pairs[:, :, :, :, 0]
@@ -223,8 +244,11 @@ def tile_gatedattentionunit_pa_kernel(
             nc.vector.tensor_tensor(out=t4[:], in0=odd, in1=cb, op=ALU.mult)
             nc.vector.tensor_tensor(out=o[:, :, :, 0:HALF], in0=t1[:], in1=t2[:], op=ALU.subtract)
             nc.vector.tensor_tensor(out=o[:, :, :, HALF:D], in0=t3[:], in1=t4[:], op=ALU.add)
+            rots[mg] = o
+
+        def store_qk(mg):
             for s in range(2):
-                nc.gpsimd.dma_start(out=qk_hbm[s][:, 4 * mg : 4 * mg + 4, :], in_=o[:, s, :, :])
+                nc.sync.dma_start(out=qk_hbm[s][:, 4 * mg : 4 * mg + 4, :], in_=rots[mg][:, s, :, :])
 
         transpose_x(0)
         copy_x(0)
@@ -242,6 +266,9 @@ def tile_gatedattentionunit_pa_kernel(
         mx(1, 0)
         mx(2, 0)
         mx(3, 0)
+        for m in (4, 5, 6, 7):
+            if m in PRE:
+                sort_x(m)
         for m in (0, 1):
             mx(m, 1)
             mx(m, 2)
@@ -258,24 +285,27 @@ def tile_gatedattentionunit_pa_kernel(
         quant_x(6)
         quant_x(7)
         nc.vector.tensor_copy(out=gains[:].rearrange("p s d -> p (s d)"), in_=gb[:, 0 : 2 * D])
-        for m in (2, 3):
-            mx(m, 1)
-            mx(m, 2)
+        mx(2, 1)
+        mx(2, 2)
         mx_qk(0)
+        mx(3, 1)
+        mx(3, 2)
+        mx_qk(1)
         for j in (3, 4, 5):
             mx(0, j)
-        mx_qk(1)
-        for m in (1, 2):
-            for j in (3, 4, 5):
-                mx(m, j)
         tb0 = back_transpose(0)
         tb1 = back_transpose(1)
         apply_gains(0, tb0)
         apply_gains(1, tb1)
-        for j in (3, 4, 5):
-            mx(3, j)
         rotate(0)
         rotate(1)
+        for m in (1, 2, 3):
+            for j in (3, 4, 5):
+                mx(m, j)
+            if m == 2:
+                store_qk(0)
         for m in (4, 5, 6, 7):
             for j in range(6):
                 mx(m, j)
+            if m == 4:
+                store_qk(1)

@@ -22,6 +22,7 @@ HALF = D // 2
 
 FLOPS = 2 * S * H * (2 * E + D)
 
+ALIGN = 256
 MANUAL = True
 BY_R = True
 PRE = (4, 5, 6, 7)
@@ -69,10 +70,10 @@ def tile_gatedattentionunit_pa_kernel(
         planes = []
         words = []
         for c, (c0, c1) in enumerate(CHUNKS):
-            plane = const.tile([P, G, c1 - c0], U8, name="plane%d" % c, align_bytes=64)
+            plane = const.tile([P, G, c1 - c0], U8, name="plane%d" % c, align_bytes=ALIGN)
             nc.vector.memset(plane[:].bitcast(I32), 0)
             planes.append(plane)
-            wtile = const.tile([P, G, 2 * (c1 - c0)], U8, name="words%d" % c, align_bytes=64)
+            wtile = const.tile([P, G, 2 * (c1 - c0)], U8, name="words%d" % c, align_bytes=ALIGN)
             words.append(wtile)
 
         ident = const.tile([P, P], F32, name="ident")
@@ -82,15 +83,15 @@ def tile_gatedattentionunit_pa_kernel(
 
         xc = const.tile([P, G, S], U32, name="xc", align_bytes=64)
         xs = const.tile([P, G, S], U8, name="xs", align_bytes=64)
-        cos_sb = const.tile([P, MT, HALF], BF16, name="cos_sb")
-        sin_sb = const.tile([P, MT, HALF], BF16, name="sin_sb")
+        cos_sb = const.tile([P, MT, HALF], BF16, name="cos_sb", align_bytes=ALIGN)
+        sin_sb = const.tile([P, MT, HALF], BF16, name="sin_sb", align_bytes=ALIGN)
         gains = const.tile([P, 2, D], F32, name="gains")
 
         xsrc = {}
 
         def load_x(i):
             m0, n = XLOADS[i]
-            xt = const.tile([P, n, H], BF16, name="x%d" % m0)
+            xt = const.tile([P, n, H], BF16, name="x%d" % m0, align_bytes=ALIGN)
             nc.sync.dma_start(out=xt[:], in_=x_hbm[:, m0 : m0 + n, :])
             for k in range(n):
                 xsrc[m0 + k] = xt[:, k, :]
@@ -176,7 +177,7 @@ def tile_gatedattentionunit_pa_kernel(
                 )
             h, jj = divmod(j, 3)
             if jj == 0:
-                ot = const.tile([P, E], F32, name="o%d_%d" % (m, h))
+                ot = const.tile([P, E], F32, name="o%d_%d" % (m, h), align_bytes=ALIGN)
                 outs[(m, h)] = ot
             ot = outs[(m, h)]
             nc.scalar.activation(out=ot[:, NT * jj : NT * (jj + 1)], in_=acc[:], func=ACT.Silu)
@@ -233,7 +234,7 @@ def tile_gatedattentionunit_pa_kernel(
             shape = [P, 2, 4, HALF]
             cb = cos_sb[:, 4 * mg : 4 * mg + 4, :].unsqueeze(1).to_broadcast(shape)
             sb = sin_sb[:, 4 * mg : 4 * mg + 4, :].unsqueeze(1).to_broadcast(shape)
-            o = ep.tile([P, 2, 4, D], F32, name="rot%d" % mg, tag="rot")
+            o = ep.tile([P, 2, 4, D], F32, name="rot%d" % mg, tag="rot", align_bytes=ALIGN)
             t1 = ep.tile(shape, F32, name="t1_%d" % mg, tag="t1")
             t2 = ep.tile(shape, F32, name="t2_%d" % mg, tag="t2")
             t3 = ep.tile(shape, F32, name="t3_%d" % mg, tag="t3")

@@ -161,6 +161,7 @@ def tile_gatedattentionunit_pa_kernel(
                 )
 
         outs = {}
+        late = []
 
         def mx(m, j):
             c, off = chunk_of(NT * j)
@@ -184,8 +185,14 @@ def tile_gatedattentionunit_pa_kernel(
             if m == MT - 1 and h == 1:
                 lo = NT * jj
                 nc.sync.dma_start(out=uv_hbm[h][:, m, lo : lo + NT], in_=ot[:, lo : lo + NT])
-            elif jj == 2:
+            elif jj == 2 and h == 0:
                 nc.sync.dma_start(out=uv_hbm[h][:, m, :], in_=ot[:])
+            if late:
+                lm = late[0]
+                late.clear()
+                nc.scalar.dma_start(out=uv_hbm[1][:, lm, :], in_=outs[(lm, 1)][:])
+            if jj == 2 and h == 1 and m != MT - 1:
+                late.append(m)
 
         qkT = {}
 

@@ -28,6 +28,8 @@ BY_R = True
 PRE = (4, 5, 6, 7)
 WARM_HEAD = 0
 WARM_GAP = 0
+V_SYNC = (0, 1, 2, 3)
+SPLIT_U = (0, 1, 2, 3)
 
 CHUNKS = ((0, 512), (512, 1536), (1536, 3200))
 XLOADS = ((0, 1), (1, 1), (2, 2), (4, 2), (6, 2))
@@ -119,11 +121,11 @@ def tile_gatedattentionunit_pa_kernel(
         load_w(0)
         load_x(2)
         load_w(1)
-        load_x(3)
-        load_x(4)
         load_w(2)
         nc.sync.dma_start(out=cos_sb[:], in_=cos_hbm)
         nc.sync.dma_start(out=sin_sb[:], in_=sin_hbm)
+        load_x(3)
+        load_x(4)
 
         xts = {}
         gxs = {}
@@ -182,16 +184,22 @@ def tile_gatedattentionunit_pa_kernel(
                 outs[(m, h)] = ot
             ot = outs[(m, h)]
             nc.scalar.activation(out=ot[:, NT * jj : NT * (jj + 1)], in_=acc[:], func=ACT.Silu)
-            if m == MT - 1 and h == 1:
+            if h == 1 and m in V_SYNC and jj == 2:
+                nc.sync.dma_start(out=uv_hbm[h][:, m, :], in_=ot[:])
+            elif m == MT - 1 and h == 1:
                 lo = NT * jj
                 nc.sync.dma_start(out=uv_hbm[h][:, m, lo : lo + NT], in_=ot[:, lo : lo + NT])
+            elif h == 0 and m in SPLIT_U and jj == 0:
+                nc.sync.dma_start(out=uv_hbm[h][:, m, 0:NT], in_=ot[:, 0:NT])
+            elif h == 0 and m in SPLIT_U and jj == 2:
+                nc.sync.dma_start(out=uv_hbm[h][:, m, NT:E], in_=ot[:, NT:E])
             elif jj == 2 and h == 0:
                 nc.sync.dma_start(out=uv_hbm[h][:, m, :], in_=ot[:])
             if late:
                 lm = late[0]
                 late.clear()
                 nc.scalar.dma_start(out=uv_hbm[1][:, lm, :], in_=outs[(lm, 1)][:])
-            if jj == 2 and h == 1 and m != MT - 1:
+            if jj == 2 and h == 1 and m != MT - 1 and m not in V_SYNC:
                 late.append(m)
 
         qkT = {}
@@ -272,48 +280,56 @@ def tile_gatedattentionunit_pa_kernel(
         quant_x(2)
         quant_x(3)
         mx(1, 0)
+        mx(0, 1)
+        mx(0, 2)
         mx(2, 0)
         mx(3, 0)
-        for m in (4, 5, 6, 7):
-            if m in PRE:
-                sort_x(m)
-        for m in (0, 1):
+        for m in (1, 2, 3):
             mx(m, 1)
             mx(m, 2)
-        for m in (4, 5, 6, 7):
-            transpose_x(m)
         gb = psum.tile([P, NT], F32, name="gb", tag="bank")
         nc.tensor.matmul(out=gb[:, 0 : 2 * D], lhsT=ones[:], rhs=gain_rows[:], start=True, stop=True)
-        copy_x(4)
-        copy_x(5)
-        quant_x(4)
-        copy_x(6)
-        quant_x(5)
-        copy_x(7)
-        quant_x(6)
-        quant_x(7)
         nc.vector.tensor_copy(out=gains[:].rearrange("p s d -> p (s d)"), in_=gb[:, 0 : 2 * D])
-        mx(2, 1)
-        mx(2, 2)
+        for m in (4, 5, 6, 7):
+            sort_x(m)
         mx_qk(0)
-        mx(3, 1)
-        mx(3, 2)
-        mx_qk(1)
         for j in (3, 4, 5):
             mx(0, j)
         tb0 = back_transpose(0)
-        tb1 = back_transpose(1)
         apply_gains(0, tb0)
-        apply_gains(1, tb1)
+        for j in (3, 4, 5):
+            mx(1, j)
+        transpose_x(4)
+        transpose_x(5)
+        copy_x(4)
+        copy_x(5)
+        quant_x(4)
+        quant_x(5)
         rotate(0)
-        rotate(1)
-        for m in (1, 2, 3):
-            for j in (3, 4, 5):
-                mx(m, j)
-            if m == 2:
+        for j in (3, 4, 5):
+            mx(2, j)
+        transpose_x(6)
+        transpose_x(7)
+        copy_x(6)
+        copy_x(7)
+        quant_x(6)
+        quant_x(7)
+        for j in (3, 4, 5):
+            mx(3, j)
+        for j in range(6):
+            mx(4, j)
+            if j == 2:
                 store_qk(0)
-        for m in (4, 5, 6, 7):
+        mx_qk(1)
+        for j in (0, 1, 2):
+            mx(5, j)
+        tb1 = back_transpose(1)
+        apply_gains(1, tb1)
+        rotate(1)
+        for j in (3, 4, 5):
+            mx(5, j)
+        for m in (6, 7):
             for j in range(6):
                 mx(m, j)
-            if m == 4:
-                store_qk(1)
+                if m == 6 and j == 2:
+                    store_qk(1)

@@ -28,7 +28,7 @@ BY_R = True
 PRE = (4, 5, 6, 7)
 WARM_HEAD = 0
 WARM_GAP = 0
-V_SYNC = (0, 1, 2, 3)
+V_SYNC = (0, 1, 2, 3, 5)
 SPLIT_U = (0, 1, 2, 3)
 
 CHUNKS = ((0, 512), (512, 1536), (1536, 3200))
@@ -306,8 +306,12 @@ def tile_gatedattentionunit_pa_kernel(
         quant_x(4)
         quant_x(5)
         rotate(0)
-        for j in (3, 4, 5):
-            mx(2, j)
+        for m in (2, 3):
+            for j in (3, 4, 5):
+                mx(m, j)
+        for j in (0, 1, 2):
+            mx(4, j)
+        store_qk(0)
         transpose_x(6)
         transpose_x(7)
         copy_x(6)
@@ -315,21 +319,19 @@ def tile_gatedattentionunit_pa_kernel(
         quant_x(6)
         quant_x(7)
         for j in (3, 4, 5):
-            mx(3, j)
-        for j in range(6):
             mx(4, j)
-            if j == 2:
-                store_qk(0)
-        mx_qk(1)
         for j in (0, 1, 2):
+            mx(5, j)
+        mx_qk(1)
+        for j in (3, 4, 5):
             mx(5, j)
         tb1 = back_transpose(1)
         apply_gains(1, tb1)
         rotate(1)
+        for j in range(6):
+            mx(6, j)
+        for j in (0, 1, 2):
+            mx(7, j)
+        store_qk(1)
         for j in (3, 4, 5):
-            mx(5, j)
-        for m in (6, 7):
-            for j in range(6):
-                mx(m, j)
-                if m == 6 and j == 2:
-                    store_qk(1)
+            mx(7, j)

from contextlib import ExitStack

import concourse.mybir as mybir
from concourse.masks import make_identity

F32 = mybir.dt.float32
BF16 = mybir.dt.bfloat16
U32 = mybir.dt.uint32
U8 = mybir.dt.uint8
I32 = mybir.dt.int32
E5X4 = mybir.dt.float8_e5m2_x4
E2X4 = mybir.dt.float4_e2m1fn_x4
ACT = mybir.ActivationFunctionType
ALU = mybir.AluOpType

S, H, E, D = 1024, 1024, 1536, 128
P = 128
MT = S // P
G = H // 512
NT = 512
HALF = D // 2

FLOPS = 2 * S * H * (2 * E + D)

ALIGN = 256
MANUAL = True
BY_R = True
PRE = (4, 5, 6, 7)
WARM_HEAD = 0
WARM_GAP = 0
V_SYNC = (0, 1, 2, 3, 5)
SPLIT_U = (0, 1, 2, 3)

CHUNKS = ((0, 512), (512, 1536), (1536, 3200))
XLOADS = ((0, 1), (1, 1), (2, 2), (4, 2), (6, 2))


def chunk_of(col):
    for c, (c0, c1) in enumerate(CHUNKS):
        if c0 <= col < c1:
            return c, col - c0
    raise ValueError("column outside W_i")


def tile_gatedattentionunit_pa_kernel(
    tc, hidden_states, sin, cos, W_i_words, W_i_scales, q_scale, k_scale, out_0, out_1, out_2, out_3
):
    nc = tc.nc
    x_hbm = hidden_states.flatten_outer_dims().rearrange("(p m) k -> p m k", m=MT)
    sin_hbm = sin.flatten_outer_dims().rearrange("(p m) i -> p m i", m=MT)
    cos_hbm = cos.flatten_outer_dims().rearrange("(p m) i -> p m i", m=MT)
    uv_hbm = [o.flatten_outer_dims().rearrange("(p m) e -> p m e", m=MT) for o in (out_0, out_1)]
    qk_hbm = [o.flatten_outer_dims().rearrange("(p m) d -> p m d", m=MT) for o in (out_2, out_3)]

    with ExitStack() as ctx:
        if MANUAL:
            ctx.enter_context(tc.manual_schedule())
        const = ctx.enter_context(tc.tile_pool(name="const", bufs=1))
        stage = ctx.enter_context(tc.tile_pool(name="stage", bufs=4))
        ep = ctx.enter_context(tc.tile_pool(name="ep", bufs=2))
        psum = ctx.enter_context(tc.psum_pool(name="psum", bufs=8))

        warm_in = const.tile([P, 1], F32, name="warm_in")
        warm_out = const.tile([P, 1], F32, name="warm_out")
        nc.vector.memset(warm_in[:], 0.0)
        nc.scalar.activation(out=warm_out[:], in_=warm_in[:], func=ACT.Silu)
        ones = const.tile([P, P], BF16, name="ones")
        nc.vector.memset(ones[:], 1.0)
        gain_rows = const.tile([P, 2 * D], BF16, name="gain_rows")
        nc.vector.memset(gain_rows[:], 0.0)

        planes = []
        words = []
        for c, (c0, c1) in enumerate(CHUNKS):
            plane = const.tile([P, G, c1 - c0], U8, name="plane%d" % c, align_bytes=ALIGN)
            nc.vector.memset(plane[:].bitcast(I32), 0)
            planes.append(plane)
            wtile = const.tile([P, G, 2 * (c1 - c0)], U8, name="words%d" % c, align_bytes=ALIGN)
            words.append(wtile)

        ident = const.tile([P, P], F32, name="ident")
        make_identity(nc, ident[:])
        nc.gpsimd.dma_start(out=gain_rows[0:1, 0:D], in_=q_scale.unsqueeze(0))
        nc.gpsimd.dma_start(out=gain_rows[0:1, D : 2 * D], in_=k_scale.unsqueeze(0))

        xc = const.tile([P, G, S], U32, name="xc", align_bytes=64)
        xs = const.tile([P, G, S], U8, name="xs", align_bytes=64)
        cos_sb = const.tile([P, MT, HALF], BF16, name="cos_sb", align_bytes=ALIGN)
        sin_sb = const.tile([P, MT, HALF], BF16, name="sin_sb", align_bytes=ALIGN)
        gains = const.tile([P, 2, D], F32, name="gains")

        xsrc = {}

        def load_x(i):
            m0, n = XLOADS[i]
            xt = const.tile([P, n, H], BF16, name="x%d" % m0, align_bytes=ALIGN)
            nc.sync.dma_start(out=xt[:], in_=x_hbm[:, m0 : m0 + n, :])
            for k in range(n):
                xsrc[m0 + k] = xt[:, k, :]

        def load_w(c):
            c0, c1 = CHUNKS[c]
            for q in range(4):
                if BY_R:
                    nc.sync.dma_start(
                        out=planes[c][q : P : 32, :, :].bitcast(I32),
                        in_=W_i_scales[:, q : 16 : 4, c0:c1].rearrange("g r n -> r g n").bitcast(I32),
                    )
                else:
                    nc.sync.dma_start(
                        out=planes[c][32 * q : 32 * q + 4, :, :].bitcast(I32),
                        in_=W_i_scales[:, 4 * q : 4 * q + 4, c0:c1].rearrange("g r n -> r g n").bitcast(I32),
                    )
            nc.sync.dma_start(
                out=words[c][:].bitcast(I32),
                in_=W_i_words[:, :, 2 * c0 : 2 * c1].rearrange("g p b -> p g b").bitcast(I32),
            )

        load_x(0)
        load_x(1)
        load_w(0)
        load_x(2)
        load_w(1)
        load_w(2)
        nc.sync.dma_start(out=cos_sb[:], in_=cos_hbm)
        nc.sync.dma_start(out=sin_sb[:], in_=sin_hbm)
        load_x(3)
        load_x(4)

        xts = {}
        gxs = {}

        pres = {}

        def sort_x(m):
            pre = stage.tile([P, G, 2, P], F32, name="pre%d" % m, tag="pre")
            nc.vector.tensor_copy(out=pre[:], in_=xsrc[m].bitcast(F32).rearrange("p (g r u) -> p g u r", g=G, u=2))
            pres[m] = pre

        def transpose_x(m):
            xt = psum.tile([P, 2 * G, P], F32, name="xt%d" % m, tag="bank")
            w = xsrc[m].bitcast(F32)
            for g in range(G):
                for u in range(2):
                    if m in PRE:
                        nc.tensor.transpose(xt[:, 2 * g + u, :], pres[m][:, g, u, :], ident[:])
                    else:
                        nc.tensor.transpose(xt[:, 2 * g + u, :], w[:, 256 * g + u : 256 * (g + 1) : 2], ident[:])
            xts[m] = xt

        def copy_x(m):
            gx = stage.tile([P, G, P, 2], F32, name="gx%d" % m, tag="gx", align_bytes=64)
            nc.vector.tensor_copy(out=gx[:], in_=xts[m][:].rearrange("p (g u) r -> p g r u", u=2))
            gxs[m] = gx

        def quant_x(m):
            cols = slice(P * m, P * (m + 1))
            for g in range(G):
                nc.vector.quantize_mx(
                    out=xc[:, g, cols].bitcast(E5X4),
                    scales=xs[:, g, cols],
                    in_=gxs[m][:, g, :, :].rearrange("p r u -> p (r u)").bitcast(BF16),
                )

        outs = {}
        late = []

        def mx(m, j):
            c, off = chunk_of(NT * j)
            acc = psum.tile([P, NT], F32, name="acc%d_%d" % (m, j), tag="bank")
            for g in range(G):
                nc.tensor.matmul_mx(
                    out=acc[:],
                    lhsT=xc[:, g, P * m : P * (m + 1)].bitcast(E5X4),
                    lhsT_scale=xs[:, g, P * m : P * (m + 1)],
                    rhs=words[c][:, g, 2 * off : 2 * (off + NT)].bitcast(E2X4),
                    rhs_scale=planes[c][:, g, off : off + NT],
                    start=(g == 0),
                    stop=(g == G - 1),
                )
            h, jj = divmod(j, 3)
            if jj == 0:
                ot = const.tile([P, E], F32, name="o%d_%d" % (m, h), align_bytes=ALIGN)
                outs[(m, h)] = ot
            ot = outs[(m, h)]
            nc.scalar.activation(out=ot[:, NT * jj : NT * (jj + 1)], in_=acc[:], func=ACT.Silu)
            if h == 1 and m in V_SYNC and jj == 2:
                nc.sync.dma_start(out=uv_hbm[h][:, m, :], in_=ot[:])
            elif m == MT - 1 and h == 1:
                lo = NT * jj
                nc.sync.dma_start(out=uv_hbm[h][:, m, lo : lo + NT], in_=ot[:, lo : lo + NT])
            elif h == 0 and m in SPLIT_U and jj == 0:
                nc.sync.dma_start(out=uv_hbm[h][:, m, 0:NT], in_=ot[:, 0:NT])
            elif h == 0 and m in SPLIT_U and jj == 2:
                nc.sync.dma_start(out=uv_hbm[h][:, m, NT:E], in_=ot[:, NT:E])
            elif jj == 2 and h == 0:
                nc.sync.dma_start(out=uv_hbm[h][:, m, :], in_=ot[:])
            if late:
                lm = late[0]
                late.clear()
                nc.scalar.dma_start(out=uv_hbm[1][:, lm, :], in_=outs[(lm, 1)][:])
            if jj == 2 and h == 1 and m != MT - 1 and m not in V_SYNC:
                late.append(m)

        qkT = {}

        def mx_qk(mg):
            c, off = chunk_of(2 * E)
            acc = psum.tile([P, NT], F32, name="qkacc%d" % mg, tag="bank")
            for g in range(G):
                nc.tensor.matmul_mx(
                    out=acc[:],
                    lhsT=words[c][:, g, 2 * off : 2 * (off + D)].bitcast(E2X4),
                    lhsT_scale=planes[c][:, g, off : off + D],
                    rhs=xc[:, g, NT * mg : NT * (mg + 1)].bitcast(E5X4),
                    rhs_scale=xs[:, g, NT * mg : NT * (mg + 1)],
                    start=(g == 0),
                    stop=(g == G - 1),
                )
            st = ep.tile([P, NT], F32, name="qkT%d" % mg, tag="qkT")
            nc.scalar.activation(out=st[:], in_=acc[:], func=ACT.Silu)
            qkT[mg] = st

        ys = {}

        def back_transpose(mg):
            tb = psum.tile([P, 4, D], F32, name="tb%d" % mg, tag="bank")
            for i in range(4):
                nc.tensor.transpose(tb[:, i, :], qkT[mg][:, P * i : P * (i + 1)], ident[:])
            return tb

        def apply_gains(mg, tb):
            y = ep.tile([P, 2, 4, D], F32, name="y%d" % mg, tag="y")
            for s in range(2):
                nc.vector.tensor_tensor(
                    out=y[:, s, :, :],
                    in0=tb[:],
                    in1=gains[:, s, :].unsqueeze(1).to_broadcast([P, 4, D]),
                    op=ALU.mult,
                )
            ys[mg] = y

        rots = {}

        def rotate(mg):
            pairs = ys[mg][:].rearrange("p s m (i e) -> p s m i e", e=2)
            even = pairs[:, :, :, :, 0]
            odd = pairs[:, :, :, :, 1]
            shape = [P, 2, 4, HALF]
            cb = cos_sb[:, 4 * mg : 4 * mg + 4, :].unsqueeze(1).to_broadcast(shape)
            sb = sin_sb[:, 4 * mg : 4 * mg + 4, :].unsqueeze(1).to_broadcast(shape)
            o = ep.tile([P, 2, 4, D], F32, name="rot%d" % mg, tag="rot", align_bytes=ALIGN)
            t1 = ep.tile(shape, F32, name="t1_%d" % mg, tag="t1")
            t2 = ep.tile(shape, F32, name="t2_%d" % mg, tag="t2")
            t3 = ep.tile(shape, F32, name="t3_%d" % mg, tag="t3")
            t4 = ep.tile(shape, F32, name="t4_%d" % mg, tag="t4")
            nc.vector.tensor_tensor(out=t1[:], in0=even, in1=cb, op=ALU.mult)
            nc.vector.tensor_tensor(out=t2[:], in0=odd, in1=sb, op=ALU.mult)
            nc.vector.tensor_tensor(out=t3[:], in0=even, in1=sb, op=ALU.mult)
            nc.vector.tensor_tensor(out=t4[:], in0=odd, in1=cb, op=ALU.mult)
            nc.vector.tensor_tensor(out=o[:, :, :, 0:HALF], in0=t1[:], in1=t2[:], op=ALU.subtract)
            nc.vector.tensor_tensor(out=o[:, :, :, HALF:D], in0=t3[:], in1=t4[:], op=ALU.add)
            rots[mg] = o

        def store_qk(mg):
            for s in range(2):
                nc.sync.dma_start(out=qk_hbm[s][:, 4 * mg : 4 * mg + 4, :], in_=rots[mg][:, s, :, :])

        transpose_x(0)
        copy_x(0)
        quant_x(0)
        transpose_x(1)
        copy_x(1)
        quant_x(1)
        mx(0, 0)
        transpose_x(2)
        transpose_x(3)
        copy_x(2)
        copy_x(3)
        quant_x(2)
        quant_x(3)
        mx(1, 0)
        mx(0, 1)
        mx(0, 2)
        mx(2, 0)
        mx(3, 0)
        for m in (1, 2, 3):
            mx(m, 1)
            mx(m, 2)
        gb = psum.tile([P, NT], F32, name="gb", tag="bank")
        nc.tensor.matmul(out=gb[:, 0 : 2 * D], lhsT=ones[:], rhs=gain_rows[:], start=True, stop=True)
        nc.vector.tensor_copy(out=gains[:].rearrange("p s d -> p (s d)"), in_=gb[:, 0 : 2 * D])
        for m in (4, 5, 6, 7):
            sort_x(m)
        mx_qk(0)
        for j in (3, 4, 5):
            mx(0, j)
        tb0 = back_transpose(0)
        apply_gains(0, tb0)
        for j in (3, 4, 5):
            mx(1, j)
        transpose_x(4)
        transpose_x(5)
        copy_x(4)
        copy_x(5)
        quant_x(4)
        quant_x(5)
        rotate(0)
        for m in (2, 3):
            for j in (3, 4, 5):
                mx(m, j)
        for j in (0, 1, 2):
            mx(4, j)
        store_qk(0)
        transpose_x(6)
        transpose_x(7)
        copy_x(6)
        copy_x(7)
        quant_x(6)
        quant_x(7)
        for j in (3, 4, 5):
            mx(4, j)
        for j in (0, 1, 2):
            mx(5, j)
        mx_qk(1)
        for j in (3, 4, 5):
            mx(5, j)
        tb1 = back_transpose(1)
        apply_gains(1, tb1)
        rotate(1)
        for j in range(6):
            mx(6, j)
        for j in (0, 1, 2):
            mx(7, j)
        store_qk(1)
        for j in (3, 4, 5):
            mx(7, j)
